import numpy as np
import ml_dtypes


def mxq(x, axis, fmt="e4m3"):
    dtype, down = {"e4m3": (ml_dtypes.float8_e4m3fn, 7), "e5m2": (ml_dtypes.float8_e5m2, 14)}[fmt]
    v = np.moveaxis(np.asarray(x, np.float32).astype(ml_dtypes.bfloat16).astype(np.float64), axis, -1)
    blocks = v.reshape(v.shape[:-1] + (-1, 32))
    amax = np.abs(blocks).max(-1, keepdims=True)
    byte = np.maximum(np.where(amax > 0, np.frexp(amax)[1] - 1 + 127, 0) - down, 1)
    scale = np.exp2(byte - 127.0)
    codes = (blocks / scale).astype(np.float32).astype(dtype).astype(np.float64)
    return np.moveaxis((codes * scale).reshape(v.shape), -1, axis)


WIDE = False


def mx_kscale(k):
    if not WIDE:
        return np.ones(k)
    levels = np.array([10, -10, 5, -5, 0])
    a = np.random.permutation(np.resize(levels, k // 512 * 4)).reshape(k // 512, 4)
    idx = np.arange(k)
    return np.exp2(a[idx // 512, idx % 128 // 32])


BF16 = ml_dtypes.bfloat16


def bf(x):
    return np.asarray(x, np.float32).astype(BF16)


def f64(x):
    return np.asarray(x).astype(np.float64)


B, S, C, H, P = 8, 512, 512, 128, 512
G2, G3 = 2, 4


def softmax(z, axis):
    e = np.exp(z - z.max(axis=axis, keepdims=True))
    return e / e.sum(axis=axis, keepdims=True)


def channel_map(q, k):
    return softmax(f64(q) @ f64(k).transpose(0, 2, 1) / np.sqrt(H), -1)


def setup_inputs():
    s = mx_kscale(S)
    return {"x": bf(np.random.standard_normal((B, S, C)) * s[None, :, None]),
            "q1": bf(np.random.standard_normal((B, C, H)) * 2.0), "k1": bf(np.random.standard_normal((B, C, H)) * 2.0),
            "q2": bf(np.random.standard_normal((G2 * B, C, H)) * 2.0), "k2": bf(np.random.standard_normal((G2 * B, C, H)) * 2.0),
            "q3": bf(np.random.standard_normal((G3 * B, C, H)) * 2.0), "k3": bf(np.random.standard_normal((G3 * B, C, H)) * 2.0),
            "wv": bf(np.random.standard_normal((S, S)) * 2.0 / np.sqrt(S) / s[:, None]),
            "bv": bf(np.random.standard_normal(S) * 0.3)}


def reference(x, q1, k1, q2, k2, q3, k3, wv, bv):
    x1 = f64(x).transpose(0, 2, 1)
    a1 = channel_map(q1, k1)
    a2 = channel_map(q2, k2).reshape(B, G2, C, C).mean(axis=1)
    a3 = channel_map(q3, k3).reshape(B, G3, C, C).mean(axis=1)
    stacked = np.stack([a1, a2, a3], axis=0)
    gate = softmax(stacked, 0)
    attn = (stacked * gate).sum(axis=0)
    v = (mxq(x1, 2, "e4m3") @ mxq(f64(wv), 0, "e4m3")) + f64(bv)
    return mxq(attn, 2, "e4m3") @ mxq(v, 1, "e4m3")

@@ -1,0 +1,235 @@
+import math
+from contextlib import ExitStack
+
+import concourse.mybir as mybir
+from concourse.masks import make_identity
+
+F32 = mybir.dt.float32
+BF16 = mybir.dt.bfloat16
+U32 = mybir.dt.uint32
+U8 = mybir.dt.uint8
+FP8X4 = mybir.dt.float8_e4m3fn_x4
+ALU = mybir.AluOpType
+ACT = mybir.ActivationFunctionType
+
+P = 128
+PACK = 4
+B, S, C, H = 8, 512, 512, 128
+TILES = C // P
+SEGMENTS = (1, 2, 4)
+FIRST_MAP = (0, 1, 3)
+MAPS = sum(SEGMENTS)
+SCORE_SCALE = 1.0 / math.sqrt(H)
+
+FLOPS = 2 * B * MAPS * C * C * H + 2 * 2 * B * C * C * S
+
+
+def tile_channeldeattention_pa_t_kernel(tc, x, q1, k1, q2, k2, q3, k3, wv, bv, out):
+    nc = tc.nc
+    queries = (q1, q2, q3)
+    keys = (k1, k2, k3)
+
+    with ExitStack() as pools:
+        consts = pools.enter_context(tc.tile_pool(name="consts", bufs=1))
+        loads = pools.enter_context(tc.tile_pool(name="loads", bufs=2))
+        values = pools.enter_context(tc.tile_pool(name="values", bufs=2))
+        front = pools.enter_context(tc.tile_pool(name="front", bufs=2))
+        small = pools.enter_context(tc.tile_pool(name="small", bufs=3))
+        back = pools.enter_context(tc.tile_pool(name="back", bufs=1))
+        psum = pools.enter_context(tc.psum_pool(name="psum", bufs=1))
+
+        ident_bf = consts.tile([P, P], BF16)
+        make_identity(nc, ident_bf)
+        ident_f32 = consts.tile([P, P], F32)
+        make_identity(nc, ident_f32)
+        bias = consts.tile([P, S], BF16)
+        nc.sync.dma_start(out=bias, in_=bv.partition_broadcast(P))
+        segments_of_map = consts.tile([P, MAPS], F32)
+        for scale, first in enumerate(FIRST_MAP):
+            nc.vector.memset(segments_of_map[:, first : first + SEGMENTS[scale]], float(SEGMENTS[scale]))
+
+        def quantise_time_major(rows, regroup, codes, scales):
+            raw = values.tile([P, PACK, C], BF16, tag="raw")
+            nc.sync.dma_start(out=raw, in_=rows.rearrange("(p s) c -> p s c", s=PACK))
+            grouped = values.tile([P, C * PACK], BF16, tag="grouped", align_bytes=64)
+            view = regroup(raw)
+            nc.vector.tensor_copy(out=grouped.rearrange("p (a b s) -> p a b s", a=view.shape[1], s=PACK), in_=view)
+            nc.vector.quantize_mx(out=codes.bitcast(FP8X4), scales=scales, in_=grouped)
+
+        wv_codes = consts.tile([P, S], U32, align_bytes=64)
+        wv_scales = consts.tile([P, S], U8, align_bytes=64)
+        quantise_time_major(wv, lambda raw: raw.rearrange("p s (a n) -> p a n s", a=1), wv_codes, wv_scales)
+
+        def prepare_values(b):
+            x_codes = values.tile([P, C], U32, align_bytes=64)
+            x_scales = values.tile([P, C], U8, align_bytes=64)
+            quantise_time_major(x[b], lambda raw: raw.rearrange("p s (m t) -> p t m s", t=PACK), x_codes, x_scales)
+
+            v_grouped = values.tile([P, S, PACK], BF16, align_bytes=64)
+            for n in range(S // P):
+                steps = slice(n * P, (n + 1) * P)
+                v_ps = psum.tile([P, PACK, P], F32, tag="v")
+                for t in range(PACK):
+                    block = slice(t * P, (t + 1) * P)
+                    nc.tensor.matmul_mx(
+                        out=v_ps[:, t, :],
+                        lhsT=x_codes[:, block].bitcast(FP8X4),
+                        lhsT_scale=x_scales[:, block],
+                        rhs=wv_codes[:, steps].bitcast(FP8X4),
+                        rhs_scale=wv_scales[:, steps],
+                        start=True,
+                        stop=True,
+                    )
+                nc.vector.tensor_tensor(
+                    out=v_grouped[:, steps, :],
+                    in0=v_ps.rearrange("p t n -> p n t"),
+                    in1=bias[:, steps].unsqueeze(2).to_broadcast([P, P, PACK]),
+                    op=ALU.add,
+                )
+            v_codes = values.tile([P, S], U32, align_bytes=64)
+            v_scales = values.tile([P, S], U8, align_bytes=64)
+            nc.vector.quantize_mx(
+                out=v_codes.bitcast(FP8X4), scales=v_scales, in_=v_grouped.rearrange("p n t -> p (n t)")
+            )
+            return v_codes, v_scales
+
+        def transpose_queries_and_keys(b):
+            raw = loads.tile([P, 2 * MAPS, TILES * H], BF16, tag="qk_raw")
+            for scale, first in enumerate(FIRST_MAP):
+                count = SEGMENTS[scale]
+                for side, source in enumerate((queries[scale], keys[scale])):
+                    nc.sync.dma_start(
+                        out=raw[:, side * MAPS + first : side * MAPS + first + count, :],
+                        in_=source[b * count : (b + 1) * count].rearrange("g (p j) h -> p g (j h)", j=TILES),
+                    )
+            qk_t = loads.tile([P, MAPS, 2 * C], BF16, tag="qk_t")
+            for m in range(MAPS):
+                t_ps = psum.tile([P, 2 * TILES, P], BF16, tag="qk_t_ps")
+                for side in range(2):
+                    for j in range(TILES):
+                        nc.tensor.transpose(
+                            t_ps[:, side * TILES + j, :], raw[:, side * MAPS + m, j * H : (j + 1) * H], ident_bf
+                        )
+                nc.scalar.copy(out=qk_t[:, m, :], in_=t_ps.rearrange("p a c -> p (a c)"))
+            return qk_t
+
+        def gate_terms(qk_t, j):
+            expo = front.tile([P, MAPS, C], F32, tag="expo")
+            neg_max = small.tile([P, MAPS], F32, tag="neg_max")
+            sums = small.tile([P, MAPS], F32, tag="sums")
+            for m in range(MAPS):
+                score = psum.tile([P, C], F32, tag="score", bufs=2)
+                nc.tensor.matmul(
+                    out=score, lhsT=qk_t[:, m, j * P : (j + 1) * P], rhs=qk_t[:, m, C : 2 * C], start=True, stop=True
+                )
+                negated = front.tile([P, C], F32, tag="negated", bufs=4)
+                nc.vector.tensor_scalar(
+                    out=negated,
+                    in0=score,
+                    scalar1=-SCORE_SCALE,
+                    scalar2=None,
+                    op0=ALU.mult,
+                    op1=ALU.min,
+                    accum_out=neg_max[:, m : m + 1],
+                )
+                nc.scalar.activation(
+                    out=expo[:, m, :],
+                    in_=negated,
+                    func=ACT.Exp,
+                    bias=neg_max[:, m : m + 1],
+                    scale=-1.0,
+                    accum_out=sums[:, m : m + 1],
+                )
+            divisor = small.tile([P, MAPS], F32, tag="divisor")
+            nc.vector.tensor_tensor(out=divisor, in0=sums, in1=segments_of_map, op=ALU.mult)
+            weight = small.tile([P, MAPS], F32, tag="weight")
+            nc.vector.reciprocal(out=weight, in_=divisor)
+            relative = small.tile([P, MAPS], F32, tag="relative")
+            for scale, first in enumerate(FIRST_MAP):
+                if SEGMENTS[scale] > 1:
+                    others = slice(first + 1, first + SEGMENTS[scale])
+                    nc.vector.tensor_scalar_mul(
+                        out=relative[:, others], in0=weight[:, others], scalar1=divisor[:, first : first + 1]
+                    )
+                    for m in range(first + 1, first + SEGMENTS[scale]):
+                        nc.vector.scalar_tensor_tensor(
+                            out=expo[:, first, :],
+                            in0=expo[:, m, :],
+                            scalar=relative[:, m : m + 1],
+                            in1=expo[:, first, :],
+                            op0=ALU.mult,
+                            op1=ALU.add,
+                        )
+            gate = front.tile([P, len(SEGMENTS), C], F32, tag="gate", bufs=6)
+            gated = front.tile([P, len(SEGMENTS), C], F32, tag="gated", bufs=6)
+            for scale, first in enumerate(FIRST_MAP):
+                nc.scalar.activation(
+                    out=gate[:, scale, :], in_=expo[:, first, :], func=ACT.Exp, scale=weight[:, first : first + 1]
+                )
+                nc.vector.scalar_tensor_tensor(
+                    out=gated[:, scale, :],
+                    in0=expo[:, first, :],
+                    scalar=weight[:, first : first + 1],
+                    in1=gate[:, scale, :],
+                    op0=ALU.mult,
+                    op1=ALU.mult,
+                )
+            return gate, gated
+
+        def sum_over_scales_transposed(terms):
+            total = psum.tile([P, PACK, P], F32, tag="total", bufs=4)
+            for t in range(PACK):
+                for scale in range(len(SEGMENTS)):
+                    nc.tensor.matmul(
+                        out=total[:, t, :],
+                        lhsT=terms[:, scale, t * P : (t + 1) * P],
+                        rhs=ident_f32,
+                        is_transpose=True,
+                        start=(scale == 0),
+                        stop=(scale == len(SEGMENTS) - 1),
+                    )
+            return total
+
+        for b in range(B):
+            v_codes, v_scales = prepare_values(b)
+            qk_t = transpose_queries_and_keys(b)
+            terms = [gate_terms(qk_t, j) for j in range(TILES)]
+
+            inverse = back.tile([P, TILES, P, PACK], F32, tag="inverse")
+            for j in range(TILES):
+                gate_sum = sum_over_scales_transposed(terms[j][0])
+                nc.scalar.activation(out=inverse[:, j, :, :], in_=gate_sum.rearrange("p t c -> p c t"), func=ACT.Ln)
+            flat_inverse = inverse.rearrange("p j c t -> p (j c t)")
+            nc.scalar.activation(out=flat_inverse, in_=flat_inverse, func=ACT.Exp, scale=-1.0)
+
+            attn_grouped = back.tile([P, TILES, P, PACK], BF16, tag="attn_grouped", align_bytes=64)
+            for j in range(TILES):
+                gated_sum = sum_over_scales_transposed(terms[j][1])
+                nc.vector.tensor_tensor(
+                    out=attn_grouped[:, j, :, :],
+                    in0=gated_sum.rearrange("p t c -> p c t"),
+                    in1=inverse[:, j, :, :],
+                    op=ALU.mult,
+                )
+            attn_codes = back.tile([P, C], U32, tag="attn_codes", align_bytes=64)
+            attn_scales = back.tile([P, C], U8, tag="attn_scales", align_bytes=64)
+            nc.vector.quantize_mx(
+                out=attn_codes.bitcast(FP8X4), scales=attn_scales, in_=attn_grouped.rearrange("p j c t -> p (j c t)")
+            )
+
+            rows_of_tile = out[b].rearrange("(p j) n -> p j n", j=TILES)
+            for j in range(TILES):
+                block = slice(j * P, (j + 1) * P)
+                result_ps = psum.tile([P, S], F32, tag="total", bufs=4)
+                nc.tensor.matmul_mx(
+                    out=result_ps,
+                    lhsT=attn_codes[:, block].bitcast(FP8X4),
+                    lhsT_scale=attn_scales[:, block],
+                    rhs=v_codes.bitcast(FP8X4),
+                    rhs_scale=v_scales,
+                    start=True,
+                    stop=True,
+                )
+                result = back.tile([P, S], F32, tag="result", bufs=3)
+                nc.scalar.copy(out=result, in_=result_ps)
+                nc.sync.dma_start(out=rows_of_tile[:, j, :], in_=result)

@@ -21,6 +21,7 @@ FIRST_MAP = (0, 1, 3)
 MAPS = sum(SEGMENTS)
 SCORE_SCALE = 1.0 / math.sqrt(H)
 
+STEPS = B * TILES
 FLOPS = 2 * B * MAPS * C * C * H + 2 * 2 * B * C * C * S
 
 
@@ -28,72 +29,23 @@ def tile_channeldeattention_pa_t_kernel(tc, x, q1, k1, q2, k2, q3, k3, wv, bv, o
     nc = tc.nc
     queries = (q1, q2, q3)
     keys = (k1, k2, k3)
+    scales_count = len(SEGMENTS)
 
     with ExitStack() as pools:
         consts = pools.enter_context(tc.tile_pool(name="consts", bufs=1))
         loads = pools.enter_context(tc.tile_pool(name="loads", bufs=2))
         values = pools.enter_context(tc.tile_pool(name="values", bufs=2))
         front = pools.enter_context(tc.tile_pool(name="front", bufs=2))
-        small = pools.enter_context(tc.tile_pool(name="small", bufs=3))
-        back = pools.enter_context(tc.tile_pool(name="back", bufs=1))
+        small = pools.enter_context(tc.tile_pool(name="small", bufs=4))
+        back = pools.enter_context(tc.tile_pool(name="back", bufs=2))
         psum = pools.enter_context(tc.psum_pool(name="psum", bufs=1))
+        pools.enter_context(tc.manual_schedule())
 
-        ident_bf = consts.tile([P, P], BF16)
-        make_identity(nc, ident_bf)
-        ident_f32 = consts.tile([P, P], F32)
-        make_identity(nc, ident_f32)
-        bias = consts.tile([P, S], BF16)
-        nc.sync.dma_start(out=bias, in_=bv.partition_broadcast(P))
-        segments_of_map = consts.tile([P, MAPS], F32)
-        for scale, first in enumerate(FIRST_MAP):
-            nc.vector.memset(segments_of_map[:, first : first + SEGMENTS[scale]], float(SEGMENTS[scale]))
+        qk_raw, x_raw, x_grouped, x_mx, v_grouped, v_mx, qk_t = {}, {}, {}, {}, {}, {}, {}
+        expo, row_stats, inverse_row_sums, weights, gate, gated = {}, {}, {}, {}, {}, {}
+        gate_sum, gated_sum, inverse, attn_grouped, attn_mx = {}, {}, {}, {}, {}
 
-        def quantise_time_major(rows, regroup, codes, scales):
-            raw = values.tile([P, PACK, C], BF16, tag="raw")
-            nc.sync.dma_start(out=raw, in_=rows.rearrange("(p s) c -> p s c", s=PACK))
-            grouped = values.tile([P, C * PACK], BF16, tag="grouped", align_bytes=64)
-            view = regroup(raw)
-            nc.vector.tensor_copy(out=grouped.rearrange("p (a b s) -> p a b s", a=view.shape[1], s=PACK), in_=view)
-            nc.vector.quantize_mx(out=codes.bitcast(FP8X4), scales=scales, in_=grouped)
-
-        wv_codes = consts.tile([P, S], U32, align_bytes=64)
-        wv_scales = consts.tile([P, S], U8, align_bytes=64)
-        quantise_time_major(wv, lambda raw: raw.rearrange("p s (a n) -> p a n s", a=1), wv_codes, wv_scales)
-
-        def prepare_values(b):
-            x_codes = values.tile([P, C], U32, align_bytes=64)
-            x_scales = values.tile([P, C], U8, align_bytes=64)
-            quantise_time_major(x[b], lambda raw: raw.rearrange("p s (m t) -> p t m s", t=PACK), x_codes, x_scales)
-
-            v_grouped = values.tile([P, S, PACK], BF16, align_bytes=64)
-            for n in range(S // P):
-                steps = slice(n * P, (n + 1) * P)
-                v_ps = psum.tile([P, PACK, P], F32, tag="v")
-                for t in range(PACK):
-                    block = slice(t * P, (t + 1) * P)
-                    nc.tensor.matmul_mx(
-                        out=v_ps[:, t, :],
-                        lhsT=x_codes[:, block].bitcast(FP8X4),
-                        lhsT_scale=x_scales[:, block],
-                        rhs=wv_codes[:, steps].bitcast(FP8X4),
-                        rhs_scale=wv_scales[:, steps],
-                        start=True,
-                        stop=True,
-                    )
-                nc.vector.tensor_tensor(
-                    out=v_grouped[:, steps, :],
-                    in0=v_ps.rearrange("p t n -> p n t"),
-                    in1=bias[:, steps].unsqueeze(2).to_broadcast([P, P, PACK]),
-                    op=ALU.add,
-                )
-            v_codes = values.tile([P, S], U32, align_bytes=64)
-            v_scales = values.tile([P, S], U8, align_bytes=64)
-            nc.vector.quantize_mx(
-                out=v_codes.bitcast(FP8X4), scales=v_scales, in_=v_grouped.rearrange("p n t -> p (n t)")
-            )
-            return v_codes, v_scales
-
-        def transpose_queries_and_keys(b):
+        def load_sample(b):
             raw = loads.tile([P, 2 * MAPS, TILES * H], BF16, tag="qk_raw")
             for scale, first in enumerate(FIRST_MAP):
                 count = SEGMENTS[scale]
@@ -102,134 +54,297 @@ def tile_channeldeattention_pa_t_kernel(tc, x, q1, k1, q2, k2, q3, k3, wv, bv, o
                         out=raw[:, side * MAPS + first : side * MAPS + first + count, :],
                         in_=source[b * count : (b + 1) * count].rearrange("g (p j) h -> p g (j h)", j=TILES),
                     )
-            qk_t = loads.tile([P, MAPS, 2 * C], BF16, tag="qk_t")
-            for m in range(MAPS):
-                t_ps = psum.tile([P, 2 * TILES, P], BF16, tag="qk_t_ps")
-                for side in range(2):
-                    for j in range(TILES):
-                        nc.tensor.transpose(
-                            t_ps[:, side * TILES + j, :], raw[:, side * MAPS + m, j * H : (j + 1) * H], ident_bf
-                        )
-                nc.scalar.copy(out=qk_t[:, m, :], in_=t_ps.rearrange("p a c -> p (a c)"))
-            return qk_t
+            qk_raw[b] = raw
+            series = loads.tile([P, PACK, C], BF16, tag="x_raw")
+            nc.sync.dma_start(out=series, in_=x[b].rearrange("(p s) c -> p s c", s=PACK))
+            x_raw[b] = series
 
-        def gate_terms(qk_t, j):
-            expo = front.tile([P, MAPS, C], F32, tag="expo")
-            neg_max = small.tile([P, MAPS], F32, tag="neg_max")
-            sums = small.tile([P, MAPS], F32, tag="sums")
-            for m in range(MAPS):
-                score = psum.tile([P, C], F32, tag="score", bufs=2)
-                nc.tensor.matmul(
-                    out=score, lhsT=qk_t[:, m, j * P : (j + 1) * P], rhs=qk_t[:, m, C : 2 * C], start=True, stop=True
+        load_sample(0)
+        wv_raw = consts.tile([P, PACK, S], BF16)
+        nc.sync.dma_start(out=wv_raw, in_=wv.rearrange("(p s) n -> p s n", s=PACK))
+        bias = consts.tile([P, S], BF16)
+        nc.sync.dma_start(out=bias, in_=bv.partition_broadcast(P))
+        ident_bf = consts.tile([P, P], BF16)
+        make_identity(nc, ident_bf)
+        ident_f32 = consts.tile([P, P], F32)
+        make_identity(nc, ident_f32)
+        share_of_map = consts.tile([P, MAPS], F32)
+        for scale, first in enumerate(FIRST_MAP):
+            nc.vector.memset(share_of_map[:, first : first + SEGMENTS[scale]], 1.0 / SEGMENTS[scale])
+        wv_grouped = consts.tile([P, S, PACK], BF16, align_bytes=64)
+        nc.vector.tensor_copy(out=wv_grouped, in_=wv_raw.rearrange("p s n -> p n s"))
+        wv_codes = consts.tile([P, S], U32, align_bytes=64)
+        wv_scales = consts.tile([P, S], U8, align_bytes=64)
+        nc.vector.quantize_mx(
+            out=wv_codes.bitcast(FP8X4), scales=wv_scales, in_=wv_grouped.rearrange("p n s -> p (n s)")
+        )
+
+        def regroup_x(b):
+            grouped = values.tile([P, PACK, P, PACK], BF16, tag="x_grouped", align_bytes=64)
+            nc.gpsimd.tensor_scalar(
+                out=grouped,
+                in0=x_raw[b].rearrange("p s (m t) -> p t m s", t=PACK),
+                scalar1=1.0,
+                scalar2=0.0,
+                op0=ALU.mult,
+                op1=ALU.add,
+            )
+            x_grouped[b] = grouped
+
+        def quantise_x(b):
+            codes = values.tile([P, C], U32, tag="x_codes", align_bytes=64)
+            scales = values.tile([P, C], U8, tag="x_scales", align_bytes=64)
+            nc.vector.quantize_mx(
+                out=codes.bitcast(FP8X4), scales=scales, in_=x_grouped[b].rearrange("p t m s -> p (t m s)")
+            )
+            x_mx[b] = (codes, scales)
+
+        def project_values(b, n):
+            if n == 0:
+                grouped = values.tile([P, S, PACK], BF16, tag="v_grouped", align_bytes=64)
+                v_grouped[b] = grouped
+            steps = slice(n * P, (n + 1) * P)
+            codes, scales = x_mx[b]
+            v_ps = psum.tile([P, PACK, P], F32, tag="v")
+            for t in range(PACK):
+                block = slice(t * P, (t + 1) * P)
+                nc.tensor.matmul_mx(
+                    out=v_ps[:, t, :],
+                    lhsT=codes[:, block].bitcast(FP8X4),
+                    lhsT_scale=scales[:, block],
+                    rhs=wv_codes[:, steps].bitcast(FP8X4),
+                    rhs_scale=wv_scales[:, steps],
+                    start=True,
+                    stop=True,
                 )
-                negated = front.tile([P, C], F32, tag="negated", bufs=4)
-                nc.vector.tensor_scalar(
-                    out=negated,
-                    in0=score,
-                    scalar1=-SCORE_SCALE,
-                    scalar2=None,
-                    op0=ALU.mult,
-                    op1=ALU.min,
-                    accum_out=neg_max[:, m : m + 1],
-                )
-                nc.scalar.activation(
-                    out=expo[:, m, :],
-                    in_=negated,
-                    func=ACT.Exp,
-                    bias=neg_max[:, m : m + 1],
-                    scale=-1.0,
-                    accum_out=sums[:, m : m + 1],
-                )
-            divisor = small.tile([P, MAPS], F32, tag="divisor")
-            nc.vector.tensor_tensor(out=divisor, in0=sums, in1=segments_of_map, op=ALU.mult)
-            weight = small.tile([P, MAPS], F32, tag="weight")
-            nc.vector.reciprocal(out=weight, in_=divisor)
+            nc.vector.tensor_tensor(
+                out=v_grouped[b][:, steps, :],
+                in0=v_ps.rearrange("p t n -> p n t"),
+                in1=bias[:, steps].unsqueeze(2).to_broadcast([P, P, PACK]),
+                op=ALU.add,
+            )
+
+        def quantise_v(b):
+            codes = values.tile([P, S], U32, tag="v_codes", align_bytes=64)
+            scales = values.tile([P, S], U8, tag="v_scales", align_bytes=64)
+            nc.vector.quantize_mx(
+                out=codes.bitcast(FP8X4), scales=scales, in_=v_grouped[b].rearrange("p n t -> p (n t)")
+            )
+            v_mx[b] = (codes, scales)
+
+        def transpose_map(b, m):
+            if m == 0:
+                turned = loads.tile([P, MAPS, 2 * C], BF16, tag="qk_t")
+                qk_t[b] = turned
+            t_ps = psum.tile([P, 2 * TILES, P], BF16, tag="qk_t_ps", bufs=2)
+            for side in range(2):
+                for j in range(TILES):
+                    nc.tensor.transpose(
+                        t_ps[:, side * TILES + j, :], qk_raw[b][:, side * MAPS + m, j * H : (j + 1) * H], ident_bf
+                    )
+            nc.scalar.copy(out=qk_t[b][:, m, :], in_=t_ps.rearrange("p a c -> p (a c)"))
+
+        def score_pass(k, m):
+            b, j = divmod(k, TILES)
+            if m == 0:
+                exponentials = front.tile([P, MAPS, C], F32, tag="expo", bufs=3)
+                neg_max = small.tile([P, MAPS], F32, tag="neg_max")
+                sums = small.tile([P, MAPS], F32, tag="sums")
+                expo[k] = exponentials
+                row_stats[k] = (neg_max, sums)
+            neg_max, sums = row_stats[k]
+            score = psum.tile([P, C], F32, tag="score", bufs=2)
+            nc.tensor.matmul(
+                out=score, lhsT=qk_t[b][:, m, j * P : (j + 1) * P], rhs=qk_t[b][:, m, C : 2 * C], start=True, stop=True
+            )
+            negated = front.tile([P, C], F32, tag="negated", bufs=3)
+            nc.vector.tensor_scalar(
+                out=negated,
+                in0=score,
+                scalar1=-SCORE_SCALE,
+                scalar2=None,
+                op0=ALU.mult,
+                op1=ALU.min,
+                accum_out=neg_max[:, m : m + 1],
+            )
+            nc.scalar.activation(
+                out=expo[k][:, m, :],
+                in_=negated,
+                func=ACT.Exp,
+                bias=neg_max[:, m : m + 1],
+                scale=-1.0,
+                accum_out=sums[:, m : m + 1],
+            )
+
+        def invert_row_sums(k):
+            inverse_sums = small.tile([P, MAPS], F32, tag="inverse_sums")
+            nc.vector.reciprocal(out=inverse_sums, in_=row_stats[k][1])
+            inverse_row_sums[k] = inverse_sums
+
+        def map_weights(k):
+            inverse_sums = inverse_row_sums[k]
+            sums = row_stats[k][1]
             relative = small.tile([P, MAPS], F32, tag="relative")
             for scale, first in enumerate(FIRST_MAP):
                 if SEGMENTS[scale] > 1:
                     others = slice(first + 1, first + SEGMENTS[scale])
                     nc.vector.tensor_scalar_mul(
-                        out=relative[:, others], in0=weight[:, others], scalar1=divisor[:, first : first + 1]
+                        out=relative[:, others], in0=inverse_sums[:, others], scalar1=sums[:, first : first + 1]
                     )
-                    for m in range(first + 1, first + SEGMENTS[scale]):
-                        nc.vector.scalar_tensor_tensor(
-                            out=expo[:, first, :],
-                            in0=expo[:, m, :],
-                            scalar=relative[:, m : m + 1],
-                            in1=expo[:, first, :],
-                            op0=ALU.mult,
-                            op1=ALU.add,
-                        )
-            gate = front.tile([P, len(SEGMENTS), C], F32, tag="gate", bufs=6)
-            gated = front.tile([P, len(SEGMENTS), C], F32, tag="gated", bufs=6)
-            for scale, first in enumerate(FIRST_MAP):
-                nc.scalar.activation(
-                    out=gate[:, scale, :], in_=expo[:, first, :], func=ACT.Exp, scale=weight[:, first : first + 1]
-                )
-                nc.vector.scalar_tensor_tensor(
-                    out=gated[:, scale, :],
-                    in0=expo[:, first, :],
-                    scalar=weight[:, first : first + 1],
-                    in1=gate[:, scale, :],
-                    op0=ALU.mult,
-                    op1=ALU.mult,
-                )
-            return gate, gated
+            weight = small.tile([P, MAPS], F32, tag="weight")
+            nc.vector.tensor_tensor(out=weight, in0=inverse_sums, in1=share_of_map, op=ALU.mult)
+            weights[k] = (weight, relative)
 
-        def sum_over_scales_transposed(terms):
-            total = psum.tile([P, PACK, P], F32, tag="total", bufs=4)
-            for t in range(PACK):
-                for scale in range(len(SEGMENTS)):
-                    nc.tensor.matmul(
-                        out=total[:, t, :],
-                        lhsT=terms[:, scale, t * P : (t + 1) * P],
-                        rhs=ident_f32,
-                        is_transpose=True,
-                        start=(scale == 0),
-                        stop=(scale == len(SEGMENTS) - 1),
-                    )
-            return total
-
-        for b in range(B):
-            v_codes, v_scales = prepare_values(b)
-            qk_t = transpose_queries_and_keys(b)
-            terms = [gate_terms(qk_t, j) for j in range(TILES)]
-
-            inverse = back.tile([P, TILES, P, PACK], F32, tag="inverse")
-            for j in range(TILES):
-                gate_sum = sum_over_scales_transposed(terms[j][0])
-                nc.scalar.activation(out=inverse[:, j, :, :], in_=gate_sum.rearrange("p t c -> p c t"), func=ACT.Ln)
-            flat_inverse = inverse.rearrange("p j c t -> p (j c t)")
-            nc.scalar.activation(out=flat_inverse, in_=flat_inverse, func=ACT.Exp, scale=-1.0)
-
-            attn_grouped = back.tile([P, TILES, P, PACK], BF16, tag="attn_grouped", align_bytes=64)
-            for j in range(TILES):
-                gated_sum = sum_over_scales_transposed(terms[j][1])
-                nc.vector.tensor_tensor(
-                    out=attn_grouped[:, j, :, :],
-                    in0=gated_sum.rearrange("p t c -> p c t"),
-                    in1=inverse[:, j, :, :],
-                    op=ALU.mult,
-                )
-            attn_codes = back.tile([P, C], U32, tag="attn_codes", align_bytes=64)
-            attn_scales = back.tile([P, C], U8, tag="attn_scales", align_bytes=64)
-            nc.vector.quantize_mx(
-                out=attn_codes.bitcast(FP8X4), scales=attn_scales, in_=attn_grouped.rearrange("p j c t -> p (j c t)")
+        def add_segment(k, scale, segment):
+            first = FIRST_MAP[scale]
+            m = first + segment
+            nc.vector.scalar_tensor_tensor(
+                out=expo[k][:, first, :],
+                in0=expo[k][:, m, :],
+                scalar=weights[k][1][:, m : m + 1],
+                in1=expo[k][:, first, :],
+                op0=ALU.mult,
+                op1=ALU.add,
             )
 
-            rows_of_tile = out[b].rearrange("(p j) n -> p j n", j=TILES)
-            for j in range(TILES):
-                block = slice(j * P, (j + 1) * P)
-                result_ps = psum.tile([P, S], F32, tag="total", bufs=4)
-                nc.tensor.matmul_mx(
-                    out=result_ps,
-                    lhsT=attn_codes[:, block].bitcast(FP8X4),
-                    lhsT_scale=attn_scales[:, block],
-                    rhs=v_codes.bitcast(FP8X4),
-                    rhs_scale=v_scales,
-                    start=True,
-                    stop=True,
+        def gate_exponential(k, scale):
+            if scale == 0:
+                exponentials = front.tile([P, scales_count, C], F32, tag="gate")
+                gate[k] = exponentials
+            first = FIRST_MAP[scale]
+            nc.scalar.activation(
+                out=gate[k][:, scale, :], in_=expo[k][:, first, :], func=ACT.Exp, scale=weights[k][0][:, first : first + 1]
+            )
+
+        def gated_map(k, scale):
+            if scale == 0:
+                products = front.tile([P, scales_count, C], F32, tag="gated")
+                gated[k] = products
+            first = FIRST_MAP[scale]
+            nc.vector.scalar_tensor_tensor(
+                out=gated[k][:, scale, :],
+                in0=expo[k][:, first, :],
+                scalar=weights[k][0][:, first : first + 1],
+                in1=gate[k][:, scale, :],
+                op0=ALU.mult,
+                op1=ALU.mult,
+            )
+
+        def add_scales_transposed(total, terms, t):
+            for scale in range(scales_count):
+                nc.tensor.matmul(
+                    out=total[:, t, :],
+                    lhsT=terms[:, scale, t * P : (t + 1) * P],
+                    rhs=ident_f32,
+                    is_transpose=True,
+                    start=(scale == 0),
+                    stop=(scale == scales_count - 1),
                 )
-                result = back.tile([P, S], F32, tag="result", bufs=3)
-                nc.scalar.copy(out=result, in_=result_ps)
-                nc.sync.dma_start(out=rows_of_tile[:, j, :], in_=result)
+
+        def sum_gates(k, t):
+            if t == 0:
+                total = psum.tile([P, PACK, P], F32, tag="gate_sum")
+                gate_sum[k] = total
+            add_scales_transposed(gate_sum[k], gate[k], t)
+
+        def sum_gated(k, t):
+            if t == 0:
+                total = psum.tile([P, PACK, P], F32, tag="gated_sum")
+                gated_sum[k] = total
+            add_scales_transposed(gated_sum[k], gated[k], t)
+
+        def log_of_gate_sum(k):
+            logs = back.tile([P, P, PACK], F32, tag="inverse")
+            nc.scalar.activation(out=logs, in_=gate_sum[k].rearrange("p t c -> p c t"), func=ACT.Ln)
+            inverse[k] = logs
+
+        def invert_gate_sum(k):
+            flat = inverse[k].rearrange("p c t -> p (c t)")
+            nc.scalar.activation(out=flat, in_=flat, func=ACT.Exp, scale=-1.0)
+
+        def fuse(k):
+            fused = back.tile([P, P, PACK], BF16, tag="attn_grouped", align_bytes=64)
+            nc.vector.tensor_tensor(
+                out=fused, in0=gated_sum[k].rearrange("p t c -> p c t"), in1=inverse[k], op=ALU.mult
+            )
+            attn_grouped[k] = fused
+
+        def quantise_attn(k):
+            codes = back.tile([P, P], U32, tag="attn_codes", align_bytes=64)
+            scales = back.tile([P, P], U8, tag="attn_scales", align_bytes=64)
+            nc.vector.quantize_mx(
+                out=codes.bitcast(FP8X4), scales=scales, in_=attn_grouped[k].rearrange("p c t -> p (c t)")
+            )
+            attn_mx[k] = (codes, scales)
+
+        def apply_attention(k):
+            b, j = divmod(k, TILES)
+            result_ps = psum.tile([P, S], F32, tag="result_ps")
+            nc.tensor.matmul_mx(
+                out=result_ps,
+                lhsT=attn_mx[k][0].bitcast(FP8X4),
+                lhsT_scale=attn_mx[k][1],
+                rhs=v_mx[b][0].bitcast(FP8X4),
+                rhs_scale=v_mx[b][1],
+                start=True,
+                stop=True,
+            )
+            result = back.tile([P, S], F32, tag="result", bufs=3)
+            nc.scalar.copy(out=result, in_=result_ps)
+            nc.sync.dma_start(out=out[b].rearrange("(p j) n -> p j n", j=TILES)[:, j, :], in_=result)
+
+        def tile_stage(stage, k, *piece):
+            if 0 <= k < STEPS:
+                stage(k, *piece)
+
+        def prepare(b, j, half):
+            if 0 <= b < B:
+                if 2 * j + half < MAPS:
+                    transpose_map(b, 2 * j + half)
+                if 0 <= 2 * j + half - 3 < S // P:
+                    project_values(b, 2 * j + half - 3)
+
+        for step in range(-TILES, STEPS + TILES):
+            b, j = divmod(step, TILES)
+            if j == 0 and b + 2 < B:
+                load_sample(b + 2)
+            if j == 0 and 0 <= b + 1 < B:
+                regroup_x(b + 1)
+            tile_stage(score_pass, step, 0)
+            tile_stage(sum_gated, step - 3, 0)
+            tile_stage(gated_map, step - 2, 2)
+            tile_stage(invert_gate_sum, step - 3)
+            tile_stage(invert_row_sums, step - 1)
+            tile_stage(score_pass, step, 1)
+            tile_stage(sum_gated, step - 3, 1)
+            prepare(b + 1, j, 0)
+            tile_stage(apply_attention, step - 4)
+            tile_stage(map_weights, step - 1)
+            tile_stage(score_pass, step, 2)
+            tile_stage(sum_gated, step - 3, 2)
+            tile_stage(add_segment, step - 1, 2, 1)
+            tile_stage(gate_exponential, step - 1, 0)
+            tile_stage(score_pass, step, 3)
+            tile_stage(sum_gated, step - 3, 3)
+            tile_stage(add_segment, step - 1, 1, 1)
+            tile_stage(add_segment, step - 1, 2, 2)
+            tile_stage(gate_exponential, step - 1, 1)
+            tile_stage(score_pass, step, 4)
+            tile_stage(sum_gates, step - 2, 0)
+            tile_stage(sum_gates, step - 2, 1)
+            tile_stage(fuse, step - 3)
+            tile_stage(add_segment, step - 1, 2, 3)
+            tile_stage(gate_exponential, step - 1, 2)
+            tile_stage(score_pass, step, 5)
+            tile_stage(sum_gates, step - 2, 2)
+            tile_stage(sum_gates, step - 2, 3)
+            prepare(b + 1, j, 1)
+            tile_stage(gated_map, step - 1, 0)
+            tile_stage(quantise_attn, step - 3)
+            tile_stage(score_pass, step, 6)
+            tile_stage(gated_map, step - 1, 1)
+            tile_stage(log_of_gate_sum, step - 2)
+            if j == 0 and 0 <= b + 1 < B:
+                quantise_x(b + 1)
+            if j == TILES - 1 and 0 <= b + 1 < B:
+                quantise_v(b + 1)

@@ -142,7 +142,7 @@ def tile_channeldeattention_pa_t_kernel(tc, x, q1, k1, q2, k2, q3, k3, wv, bv, o
                     nc.tensor.transpose(
                         t_ps[:, side * TILES + j, :], qk_raw[b][:, side * MAPS + m, j * H : (j + 1) * H], ident_bf
                     )
-            nc.scalar.copy(out=qk_t[b][:, m, :], in_=t_ps.rearrange("p a c -> p (a c)"))
+            nc.vector.tensor_copy(out=qk_t[b][:, m, :], in_=t_ps.rearrange("p a c -> p (a c)"))
 
         def score_pass(k, m):
             b, j = divmod(k, TILES)

@@ -19,6 +19,7 @@ TILES = C // P
 SEGMENTS = (1, 2, 4)
 FIRST_MAP = (0, 1, 3)
 MAPS = sum(SEGMENTS)
+PLACE = (0, 1, 3, 2, 4, 5, 6)
 SCORE_SCALE = 1.0 / math.sqrt(H)
 
 STEPS = B * TILES
@@ -41,7 +42,7 @@ def tile_channeldeattention_pa_t_kernel(tc, x, q1, k1, q2, k2, q3, k3, wv, bv, o
         psum = pools.enter_context(tc.psum_pool(name="psum", bufs=1))
         pools.enter_context(tc.manual_schedule())
 
-        qk_raw, x_raw, x_grouped, x_mx, v_grouped, v_mx, qk_t = {}, {}, {}, {}, {}, {}, {}
+        qk_raw, x_raw, x_grouped, x_mx, v_grouped, v_mx, qk_t, qk_t_ps = {}, {}, {}, {}, {}, {}, {}, {}
         expo, row_stats, inverse_row_sums, weights, gate, gated = {}, {}, {}, {}, {}, {}
         gate_sum, gated_sum, inverse, attn_grouped, attn_mx = {}, {}, {}, {}, {}
 
@@ -132,17 +133,19 @@ def tile_channeldeattention_pa_t_kernel(tc, x, q1, k1, q2, k2, q3, k3, wv, bv, o
             )
             v_mx[b] = (codes, scales)
 
-        def transpose_map(b, m):
-            if m == 0:
+        def transpose_map(b, m, side):
+            if m == 0 and side == 0:
                 turned = loads.tile([P, MAPS, 2 * C], BF16, tag="qk_t")
                 qk_t[b] = turned
-            t_ps = psum.tile([P, 2 * TILES, P], BF16, tag="qk_t_ps", bufs=2)
-            for side in range(2):
-                for j in range(TILES):
-                    nc.tensor.transpose(
-                        t_ps[:, side * TILES + j, :], qk_raw[b][:, side * MAPS + m, j * H : (j + 1) * H], ident_bf
-                    )
-            nc.vector.tensor_copy(out=qk_t[b][:, m, :], in_=t_ps.rearrange("p a c -> p (a c)"))
+            if side == 0:
+                bank = psum.tile([P, 2 * TILES, P], BF16, tag="qk_t_ps", bufs=2)
+                qk_t_ps[b] = bank
+            for j in range(TILES):
+                nc.tensor.transpose(
+                    qk_t_ps[b][:, side * TILES + j, :], qk_raw[b][:, side * MAPS + m, j * H : (j + 1) * H], ident_bf
+                )
+            if side == 1:
+                nc.scalar.copy(out=qk_t[b][:, m, :], in_=qk_t_ps[b].rearrange("p a c -> p (a c)"))
 
         def score_pass(k, m):
             b, j = divmod(k, TILES)
@@ -157,7 +160,7 @@ def tile_channeldeattention_pa_t_kernel(tc, x, q1, k1, q2, k2, q3, k3, wv, bv, o
             nc.tensor.matmul(
                 out=score, lhsT=qk_t[b][:, m, j * P : (j + 1) * P], rhs=qk_t[b][:, m, C : 2 * C], start=True, stop=True
             )
-            negated = front.tile([P, C], F32, tag="negated", bufs=3)
+            negated = front.tile([P, C], F32, tag="negated", bufs=4)
             nc.vector.tensor_scalar(
                 out=negated,
                 in0=score,
@@ -168,7 +171,7 @@ def tile_channeldeattention_pa_t_kernel(tc, x, q1, k1, q2, k2, q3, k3, wv, bv, o
                 accum_out=neg_max[:, m : m + 1],
             )
             nc.scalar.activation(
-                out=expo[k][:, m, :],
+                out=expo[k][:, PLACE[m], :],
                 in_=negated,
                 func=ACT.Exp,
                 bias=neg_max[:, m : m + 1],
@@ -182,53 +185,41 @@ def tile_channeldeattention_pa_t_kernel(tc, x, q1, k1, q2, k2, q3, k3, wv, bv, o
             inverse_row_sums[k] = inverse_sums
 
         def map_weights(k):
-            inverse_sums = inverse_row_sums[k]
-            sums = row_stats[k][1]
-            relative = small.tile([P, MAPS], F32, tag="relative")
-            for scale, first in enumerate(FIRST_MAP):
-                if SEGMENTS[scale] > 1:
-                    others = slice(first + 1, first + SEGMENTS[scale])
-                    nc.vector.tensor_scalar_mul(
-                        out=relative[:, others], in0=inverse_sums[:, others], scalar1=sums[:, first : first + 1]
-                    )
             weight = small.tile([P, MAPS], F32, tag="weight")
-            nc.vector.tensor_tensor(out=weight, in0=inverse_sums, in1=share_of_map, op=ALU.mult)
-            weights[k] = (weight, relative)
+            nc.vector.tensor_tensor(out=weight, in0=inverse_row_sums[k], in1=share_of_map, op=ALU.mult)
+            weights[k] = weight
+
+        def weigh_first_maps(k):
+            for scale, first in enumerate(FIRST_MAP):
+                nc.gpsimd.tensor_scalar(
+                    out=expo[k][:, scale, :],
+                    in0=expo[k][:, scale, :],
+                    scalar1=weights[k][:, first : first + 1],
+                    scalar2=0.0,
+                    op0=ALU.mult,
+                    op1=ALU.add,
+                )
 
         def add_segment(k, scale, segment):
-            first = FIRST_MAP[scale]
-            m = first + segment
+            m = FIRST_MAP[scale] + segment
             nc.vector.scalar_tensor_tensor(
-                out=expo[k][:, first, :],
-                in0=expo[k][:, m, :],
-                scalar=weights[k][1][:, m : m + 1],
-                in1=expo[k][:, first, :],
+                out=expo[k][:, scale, :],
+                in0=expo[k][:, PLACE[m], :],
+                scalar=weights[k][:, m : m + 1],
+                in1=expo[k][:, scale, :],
                 op0=ALU.mult,
                 op1=ALU.add,
             )
 
-        def gate_exponential(k, scale):
-            if scale == 0:
-                exponentials = front.tile([P, scales_count, C], F32, tag="gate")
-                gate[k] = exponentials
-            first = FIRST_MAP[scale]
-            nc.scalar.activation(
-                out=gate[k][:, scale, :], in_=expo[k][:, first, :], func=ACT.Exp, scale=weights[k][0][:, first : first + 1]
-            )
+        def gate_exponentials(k):
+            exponentials = front.tile([P, scales_count, C], F32, tag="gate")
+            nc.scalar.activation(out=exponentials, in_=expo[k][:, 0:scales_count, :], func=ACT.Exp)
+            gate[k] = exponentials
 
-        def gated_map(k, scale):
-            if scale == 0:
-                products = front.tile([P, scales_count, C], F32, tag="gated")
-                gated[k] = products
-            first = FIRST_MAP[scale]
-            nc.vector.scalar_tensor_tensor(
-                out=gated[k][:, scale, :],
-                in0=expo[k][:, first, :],
-                scalar=weights[k][0][:, first : first + 1],
-                in1=gate[k][:, scale, :],
-                op0=ALU.mult,
-                op1=ALU.mult,
-            )
+        def gated_maps(k):
+            products = front.tile([P, scales_count, C], F32, tag="gated")
+            nc.vector.tensor_tensor(out=products, in0=expo[k][:, 0:scales_count, :], in1=gate[k], op=ALU.mult)
+            gated[k] = products
 
         def add_scales_transposed(total, terms, t):
             for scale in range(scales_count):
@@ -297,54 +288,55 @@ def tile_channeldeattention_pa_t_kernel(tc, x, q1, k1, q2, k2, q3, k3, wv, bv, o
             if 0 <= k < STEPS:
                 stage(k, *piece)
 
-        def prepare(b, j, half):
+        def sample_stage(stage, b, *piece):
             if 0 <= b < B:
-                if 2 * j + half < MAPS:
-                    transpose_map(b, 2 * j + half)
-                if 0 <= 2 * j + half - 3 < S // P:
-                    project_values(b, 2 * j + half - 3)
+                stage(b, *piece)
 
-        for step in range(-TILES, STEPS + TILES):
+        def transpose_next(b, j, half, side):
+            if 2 * j + half < MAPS:
+                sample_stage(transpose_map, b + 1, 2 * j + half, side)
+
+        for step in range(-TILES - 1, STEPS + TILES):
             b, j = divmod(step, TILES)
-            if j == 0 and b + 2 < B:
-                load_sample(b + 2)
-            if j == 0 and 0 <= b + 1 < B:
-                regroup_x(b + 1)
+            last = TILES - 1
+            if j == 0:
+                sample_stage(load_sample, b + 2)
+            if j == last:
+                sample_stage(regroup_x, b + 2)
             tile_stage(score_pass, step, 0)
-            tile_stage(sum_gated, step - 3, 0)
-            tile_stage(gated_map, step - 2, 2)
-            tile_stage(invert_gate_sum, step - 3)
+            tile_stage(sum_gates, step - 3, 0)
+            tile_stage(sum_gates, step - 3, 1)
+            tile_stage(add_segment, step - 2, 2, 3)
+            tile_stage(fuse, step - 4)
+            tile_stage(gate_exponentials, step - 2)
             tile_stage(invert_row_sums, step - 1)
             tile_stage(score_pass, step, 1)
-            tile_stage(sum_gated, step - 3, 1)
-            prepare(b + 1, j, 0)
-            tile_stage(apply_attention, step - 4)
+            tile_stage(sum_gates, step - 3, 2)
+            tile_stage(sum_gates, step - 3, 3)
+            tile_stage(quantise_attn, step - 4)
             tile_stage(map_weights, step - 1)
+            tile_stage(weigh_first_maps, step - 1)
             tile_stage(score_pass, step, 2)
+            transpose_next(b, j, 0, 0)
+            tile_stage(log_of_gate_sum, step - 3)
+            tile_stage(score_pass, step, 3)
+            transpose_next(b, j, 0, 1)
+            tile_stage(sum_gated, step - 3, 0)
+            sample_stage(project_values, b + 1, j)
+            tile_stage(invert_gate_sum, step - 3)
+            tile_stage(score_pass, step, 4)
+            tile_stage(apply_attention, step - 4)
+            tile_stage(sum_gated, step - 3, 1)
+            tile_stage(gated_maps, step - 2)
+            tile_stage(score_pass, step, 5)
+            transpose_next(b, j, 1, 0)
             tile_stage(sum_gated, step - 3, 2)
             tile_stage(add_segment, step - 1, 2, 1)
-            tile_stage(gate_exponential, step - 1, 0)
-            tile_stage(score_pass, step, 3)
+            tile_stage(score_pass, step, 6)
+            transpose_next(b, j, 1, 1)
             tile_stage(sum_gated, step - 3, 3)
             tile_stage(add_segment, step - 1, 1, 1)
             tile_stage(add_segment, step - 1, 2, 2)
-            tile_stage(gate_exponential, step - 1, 1)
-            tile_stage(score_pass, step, 4)
-            tile_stage(sum_gates, step - 2, 0)
-            tile_stage(sum_gates, step - 2, 1)
-            tile_stage(fuse, step - 3)
-            tile_stage(add_segment, step - 1, 2, 3)
-            tile_stage(gate_exponential, step - 1, 2)
-            tile_stage(score_pass, step, 5)
-            tile_stage(sum_gates, step - 2, 2)
-            tile_stage(sum_gates, step - 2, 3)
-            prepare(b + 1, j, 1)
-            tile_stage(gated_map, step - 1, 0)
-            tile_stage(quantise_attn, step - 3)
-            tile_stage(score_pass, step, 6)
-            tile_stage(gated_map, step - 1, 1)
-            tile_stage(log_of_gate_sum, step - 2)
-            if j == 0 and 0 <= b + 1 < B:
-                quantise_x(b + 1)
-            if j == TILES - 1 and 0 <= b + 1 < B:
-                quantise_v(b + 1)
+            if j == last:
+                sample_stage(quantise_x, b + 2)
+                sample_stage(quantise_v, b + 1)

@@ -43,7 +43,7 @@ def tile_channeldeattention_pa_t_kernel(tc, x, q1, k1, q2, k2, q3, k3, wv, bv, o
         pools.enter_context(tc.manual_schedule())
 
         qk_raw, x_raw, x_grouped, x_mx, v_grouped, v_mx, qk_t, qk_t_ps = {}, {}, {}, {}, {}, {}, {}, {}
-        expo, row_stats, inverse_row_sums, weights, gate, gated = {}, {}, {}, {}, {}, {}
+        expo, row_stats, inverse_row_sums, weights, ratios, gate, gated = {}, {}, {}, {}, {}, {}, {}
         gate_sum, gated_sum, inverse, attn_grouped, attn_mx = {}, {}, {}, {}, {}
 
         def load_sample(b):
@@ -69,9 +69,10 @@ def tile_channeldeattention_pa_t_kernel(tc, x, q1, k1, q2, k2, q3, k3, wv, bv, o
         make_identity(nc, ident_bf)
         ident_f32 = consts.tile([P, P], F32)
         make_identity(nc, ident_f32)
-        share_of_map = consts.tile([P, MAPS], F32)
+        share_of_map = consts.tile([P, FIRST_MAP[-1] + 1], F32)
+        nc.vector.memset(share_of_map, 1.0)
         for scale, first in enumerate(FIRST_MAP):
-            nc.vector.memset(share_of_map[:, first : first + SEGMENTS[scale]], 1.0 / SEGMENTS[scale])
+            nc.vector.memset(share_of_map[:, first : first + 1], 1.0 / SEGMENTS[scale])
         wv_grouped = consts.tile([P, S, PACK], BF16, align_bytes=64)
         nc.vector.tensor_copy(out=wv_grouped, in_=wv_raw.rearrange("p s n -> p n s"))
         wv_codes = consts.tile([P, S], U32, align_bytes=64)
@@ -185,40 +186,61 @@ def tile_channeldeattention_pa_t_kernel(tc, x, q1, k1, q2, k2, q3, k3, wv, bv, o
             inverse_row_sums[k] = inverse_sums
 
         def map_weights(k):
-            weight = small.tile([P, MAPS], F32, tag="weight")
-            nc.vector.tensor_tensor(out=weight, in0=inverse_row_sums[k], in1=share_of_map, op=ALU.mult)
+            sums, inverse_sums = row_stats[k][1], inverse_row_sums[k]
+            weight = small.tile([P, FIRST_MAP[-1] + 1], F32, tag="weight")
+            nc.gpsimd.tensor_tensor(
+                out=weight, in0=inverse_sums[:, 0 : FIRST_MAP[-1] + 1], in1=share_of_map, op=ALU.mult
+            )
             weights[k] = weight
-
-        def weigh_first_maps(k):
-            for scale, first in enumerate(FIRST_MAP):
+            ratio = small.tile([P, MAPS], F32, tag="ratio")
+            for scale in (1, 2):
+                first = FIRST_MAP[scale]
+                others = slice(first + 1, first + SEGMENTS[scale])
                 nc.gpsimd.tensor_scalar(
-                    out=expo[k][:, scale, :],
-                    in0=expo[k][:, scale, :],
-                    scalar1=weights[k][:, first : first + 1],
-                    scalar2=0.0,
+                    out=ratio[:, others],
+                    in0=inverse_sums[:, others],
+                    scalar1=sums[:, first : first + 1],
+                    scalar2=None,
                     op0=ALU.mult,
-                    op1=ALU.add,
                 )
+            ratios[k] = ratio
 
         def add_segment(k, scale, segment):
             m = FIRST_MAP[scale] + segment
             nc.vector.scalar_tensor_tensor(
                 out=expo[k][:, scale, :],
                 in0=expo[k][:, PLACE[m], :],
-                scalar=weights[k][:, m : m + 1],
+                scalar=ratios[k][:, m : m + 1],
                 in1=expo[k][:, scale, :],
                 op0=ALU.mult,
                 op1=ALU.add,
             )
 
+        def weight_of_scale(k, scale):
+            return weights[k][:, FIRST_MAP[scale] : FIRST_MAP[scale] + 1]
+
         def gate_exponentials(k):
             exponentials = front.tile([P, scales_count, C], F32, tag="gate")
-            nc.scalar.activation(out=exponentials, in_=expo[k][:, 0:scales_count, :], func=ACT.Exp)
+            for scale in range(scales_count):
+                nc.scalar.activation(
+                    out=exponentials[:, scale, :],
+                    in_=expo[k][:, scale, :],
+                    func=ACT.Exp,
+                    scale=weight_of_scale(k, scale),
+                )
             gate[k] = exponentials
 
         def gated_maps(k):
             products = front.tile([P, scales_count, C], F32, tag="gated")
-            nc.vector.tensor_tensor(out=products, in0=expo[k][:, 0:scales_count, :], in1=gate[k], op=ALU.mult)
+            for scale in range(scales_count):
+                nc.vector.scalar_tensor_tensor(
+                    out=products[:, scale, :],
+                    in0=expo[k][:, scale, :],
+                    scalar=weight_of_scale(k, scale),
+                    in1=gate[k][:, scale, :],
+                    op0=ALU.mult,
+                    op1=ALU.mult,
+                )
             gated[k] = products
 
         def add_scales_transposed(total, terms, t):
@@ -315,7 +337,6 @@ def tile_channeldeattention_pa_t_kernel(tc, x, q1, k1, q2, k2, q3, k3, wv, bv, o
             tile_stage(sum_gates, step - 3, 3)
             tile_stage(quantise_attn, step - 4)
             tile_stage(map_weights, step - 1)
-            tile_stage(weigh_first_maps, step - 1)
             tile_stage(score_pass, step, 2)
             transpose_next(b, j, 0, 0)
             tile_stage(log_of_gate_sum, step - 3)

import math
from contextlib import ExitStack

import concourse.mybir as mybir
from concourse.masks import make_identity

F32 = mybir.dt.float32
BF16 = mybir.dt.bfloat16
U32 = mybir.dt.uint32
U8 = mybir.dt.uint8
FP8X4 = mybir.dt.float8_e4m3fn_x4
ALU = mybir.AluOpType
ACT = mybir.ActivationFunctionType

P = 128
PACK = 4
B, S, C, H = 8, 512, 512, 128
TILES = C // P
SEGMENTS = (1, 2, 4)
FIRST_MAP = (0, 1, 3)
MAPS = sum(SEGMENTS)
PLACE = (0, 1, 3, 2, 4, 5, 6)
SCORE_SCALE = 1.0 / math.sqrt(H)

STEPS = B * TILES
FLOPS = 2 * B * MAPS * C * C * H + 2 * 2 * B * C * C * S


def tile_channeldeattention_pa_t_kernel(tc, x, q1, k1, q2, k2, q3, k3, wv, bv, out):
    nc = tc.nc
    queries = (q1, q2, q3)
    keys = (k1, k2, k3)
    scales_count = len(SEGMENTS)

    with ExitStack() as pools:
        consts = pools.enter_context(tc.tile_pool(name="consts", bufs=1))
        loads = pools.enter_context(tc.tile_pool(name="loads", bufs=2))
        values = pools.enter_context(tc.tile_pool(name="values", bufs=2))
        front = pools.enter_context(tc.tile_pool(name="front", bufs=2))
        small = pools.enter_context(tc.tile_pool(name="small", bufs=4))
        back = pools.enter_context(tc.tile_pool(name="back", bufs=2))
        psum = pools.enter_context(tc.psum_pool(name="psum", bufs=1))
        pools.enter_context(tc.manual_schedule())

        qk_raw, x_raw, x_grouped, x_mx, v_grouped, v_mx, qk_t, qk_t_ps = {}, {}, {}, {}, {}, {}, {}, {}
        expo, row_stats, inverse_row_sums, weights, ratios, gate, gated = {}, {}, {}, {}, {}, {}, {}
        gate_sum, gated_sum, inverse, attn_grouped, attn_mx = {}, {}, {}, {}, {}

        def load_sample(b):
            raw = loads.tile([P, 2 * MAPS, TILES * H], BF16, tag="qk_raw")
            for scale, first in enumerate(FIRST_MAP):
                count = SEGMENTS[scale]
                for side, source in enumerate((queries[scale], keys[scale])):
                    nc.sync.dma_start(
                        out=raw[:, side * MAPS + first : side * MAPS + first + count, :],
                        in_=source[b * count : (b + 1) * count].rearrange("g (p j) h -> p g (j h)", j=TILES),
                    )
            qk_raw[b] = raw
            series = loads.tile([P, PACK, C], BF16, tag="x_raw")
            nc.sync.dma_start(out=series, in_=x[b].rearrange("(p s) c -> p s c", s=PACK))
            x_raw[b] = series

        load_sample(0)
        wv_raw = consts.tile([P, PACK, S], BF16)
        nc.sync.dma_start(out=wv_raw, in_=wv.rearrange("(p s) n -> p s n", s=PACK))
        bias = consts.tile([P, S], BF16)
        nc.sync.dma_start(out=bias, in_=bv.partition_broadcast(P))
        ident_bf = consts.tile([P, P], BF16)
        make_identity(nc, ident_bf)
        ident_f32 = consts.tile([P, P], F32)
        make_identity(nc, ident_f32)
        share_of_map = consts.tile([P, FIRST_MAP[-1] + 1], F32)
        nc.vector.memset(share_of_map, 1.0)
        for scale, first in enumerate(FIRST_MAP):
            nc.vector.memset(share_of_map[:, first : first + 1], 1.0 / SEGMENTS[scale])
        wv_grouped = consts.tile([P, S, PACK], BF16, align_bytes=64)
        nc.vector.tensor_copy(out=wv_grouped, in_=wv_raw.rearrange("p s n -> p n s"))
        wv_codes = consts.tile([P, S], U32, align_bytes=64)
        wv_scales = consts.tile([P, S], U8, align_bytes=64)
        nc.vector.quantize_mx(
            out=wv_codes.bitcast(FP8X4), scales=wv_scales, in_=wv_grouped.rearrange("p n s -> p (n s)")
        )

        def regroup_x(b):
            grouped = values.tile([P, PACK, P, PACK], BF16, tag="x_grouped", align_bytes=64)
            nc.gpsimd.tensor_scalar(
                out=grouped,
                in0=x_raw[b].rearrange("p s (m t) -> p t m s", t=PACK),
                scalar1=1.0,
                scalar2=0.0,
                op0=ALU.mult,
                op1=ALU.add,
            )
            x_grouped[b] = grouped

        def quantise_x(b):
            codes = values.tile([P, C], U32, tag="x_codes", align_bytes=64)
            scales = values.tile([P, C], U8, tag="x_scales", align_bytes=64)
            nc.vector.quantize_mx(
                out=codes.bitcast(FP8X4), scales=scales, in_=x_grouped[b].rearrange("p t m s -> p (t m s)")
            )
            x_mx[b] = (codes, scales)

        def project_values(b, n):
            if n == 0:
                grouped = values.tile([P, S, PACK], BF16, tag="v_grouped", align_bytes=64)
                v_grouped[b] = grouped
            steps = slice(n * P, (n + 1) * P)
            codes, scales = x_mx[b]
            v_ps = psum.tile([P, PACK, P], F32, tag="v")
            for t in range(PACK):
                block = slice(t * P, (t + 1) * P)
                nc.tensor.matmul_mx(
                    out=v_ps[:, t, :],
                    lhsT=codes[:, block].bitcast(FP8X4),
                    lhsT_scale=scales[:, block],
                    rhs=wv_codes[:, steps].bitcast(FP8X4),
                    rhs_scale=wv_scales[:, steps],
                    start=True,
                    stop=True,
                )
            nc.vector.tensor_tensor(
                out=v_grouped[b][:, steps, :],
                in0=v_ps.rearrange("p t n -> p n t"),
                in1=bias[:, steps].unsqueeze(2).to_broadcast([P, P, PACK]),
                op=ALU.add,
            )

        def quantise_v(b):
            codes = values.tile([P, S], U32, tag="v_codes", align_bytes=64)
            scales = values.tile([P, S], U8, tag="v_scales", align_bytes=64)
            nc.vector.quantize_mx(
                out=codes.bitcast(FP8X4), scales=scales, in_=v_grouped[b].rearrange("p n t -> p (n t)")
            )
            v_mx[b] = (codes, scales)

        def transpose_map(b, m, side):
            if m == 0 and side == 0:
                turned = loads.tile([P, MAPS, 2 * C], BF16, tag="qk_t")
                qk_t[b] = turned
            if side == 0:
                bank = psum.tile([P, 2 * TILES, P], BF16, tag="qk_t_ps", bufs=2)
                qk_t_ps[b] = bank
            for j in range(TILES):
                nc.tensor.transpose(
                    qk_t_ps[b][:, side * TILES + j, :], qk_raw[b][:, side * MAPS + m, j * H : (j + 1) * H], ident_bf
                )
            if side == 1:
                nc.scalar.copy(out=qk_t[b][:, m, :], in_=qk_t_ps[b].rearrange("p a c -> p (a c)"))

        def score_pass(k, m):
            b, j = divmod(k, TILES)
            if m == 0:
                exponentials = front.tile([P, MAPS, C], F32, tag="expo", bufs=3)
                neg_max = small.tile([P, MAPS], F32, tag="neg_max")
                sums = small.tile([P, MAPS], F32, tag="sums")
                expo[k] = exponentials
                row_stats[k] = (neg_max, sums)
            neg_max, sums = row_stats[k]
            score = psum.tile([P, C], F32, tag="score", bufs=2)
            nc.tensor.matmul(
                out=score, lhsT=qk_t[b][:, m, j * P : (j + 1) * P], rhs=qk_t[b][:, m, C : 2 * C], start=True, stop=True
            )
            negated = front.tile([P, C], F32, tag="negated", bufs=4)
            nc.vector.tensor_scalar(
                out=negated,
                in0=score,
                scalar1=-SCORE_SCALE,
                scalar2=None,
                op0=ALU.mult,
                op1=ALU.min,
                accum_out=neg_max[:, m : m + 1],
            )
            nc.scalar.activation(
                out=expo[k][:, PLACE[m], :],
                in_=negated,
                func=ACT.Exp,
                bias=neg_max[:, m : m + 1],
                scale=-1.0,
                accum_out=sums[:, m : m + 1],
            )

        def invert_row_sums(k):
            inverse_sums = small.tile([P, MAPS], F32, tag="inverse_sums")
            nc.vector.reciprocal(out=inverse_sums, in_=row_stats[k][1])
            inverse_row_sums[k] = inverse_sums

        def map_weights(k):
            sums, inverse_sums = row_stats[k][1], inverse_row_sums[k]
            weight = small.tile([P, FIRST_MAP[-1] + 1], F32, tag="weight")
            nc.gpsimd.tensor_tensor(
                out=weight, in0=inverse_sums[:, 0 : FIRST_MAP[-1] + 1], in1=share_of_map, op=ALU.mult
            )
            weights[k] = weight
            ratio = small.tile([P, MAPS], F32, tag="ratio")
            for scale in (1, 2):
                first = FIRST_MAP[scale]
                others = slice(first + 1, first + SEGMENTS[scale])
                nc.gpsimd.tensor_scalar(
                    out=ratio[:, others],
                    in0=inverse_sums[:, others],
                    scalar1=sums[:, first : first + 1],
                    scalar2=None,
                    op0=ALU.mult,
                )
            ratios[k] = ratio

        def add_segment(k, scale, segment):
            m = FIRST_MAP[scale] + segment
            nc.vector.scalar_tensor_tensor(
                out=expo[k][:, scale, :],
                in0=expo[k][:, PLACE[m], :],
                scalar=ratios[k][:, m : m + 1],
                in1=expo[k][:, scale, :],
                op0=ALU.mult,
                op1=ALU.add,
            )

        def weight_of_scale(k, scale):
            return weights[k][:, FIRST_MAP[scale] : FIRST_MAP[scale] + 1]

        def gate_exponentials(k):
            exponentials = front.tile([P, scales_count, C], F32, tag="gate")
            for scale in range(scales_count):
                nc.scalar.activation(
                    out=exponentials[:, scale, :],
                    in_=expo[k][:, scale, :],
                    func=ACT.Exp,
                    scale=weight_of_scale(k, scale),
                )
            gate[k] = exponentials

        def gated_maps(k):
            products = front.tile([P, scales_count, C], F32, tag="gated")
            for scale in range(scales_count):
                nc.vector.scalar_tensor_tensor(
                    out=products[:, scale, :],
                    in0=expo[k][:, scale, :],
                    scalar=weight_of_scale(k, scale),
                    in1=gate[k][:, scale, :],
                    op0=ALU.mult,
                    op1=ALU.mult,
                )
            gated[k] = products

        def add_scales_transposed(total, terms, t):
            for scale in range(scales_count):
                nc.tensor.matmul(
                    out=total[:, t, :],
                    lhsT=terms[:, scale, t * P : (t + 1) * P],
                    rhs=ident_f32,
                    is_transpose=True,
                    start=(scale == 0),
                    stop=(scale == scales_count - 1),
                )

        def sum_gates(k, t):
            if t == 0:
                total = psum.tile([P, PACK, P], F32, tag="gate_sum")
                gate_sum[k] = total
            add_scales_transposed(gate_sum[k], gate[k], t)

        def sum_gated(k, t):
            if t == 0:
                total = psum.tile([P, PACK, P], F32, tag="gated_sum")
                gated_sum[k] = total
            add_scales_transposed(gated_sum[k], gated[k], t)

        def log_of_gate_sum(k):
            logs = back.tile([P, P, PACK], F32, tag="inverse")
            nc.scalar.activation(out=logs, in_=gate_sum[k].rearrange("p t c -> p c t"), func=ACT.Ln)
            inverse[k] = logs

        def invert_gate_sum(k):
            flat = inverse[k].rearrange("p c t -> p (c t)")
            nc.scalar.activation(out=flat, in_=flat, func=ACT.Exp, scale=-1.0)

        def fuse(k):
            fused = back.tile([P, P, PACK], BF16, tag="attn_grouped", align_bytes=64)
            nc.vector.tensor_tensor(
                out=fused, in0=gated_sum[k].rearrange("p t c -> p c t"), in1=inverse[k], op=ALU.mult
            )
            attn_grouped[k] = fused

        def quantise_attn(k):
            codes = back.tile([P, P], U32, tag="attn_codes", align_bytes=64)
            scales = back.tile([P, P], U8, tag="attn_scales", align_bytes=64)
            nc.vector.quantize_mx(
                out=codes.bitcast(FP8X4), scales=scales, in_=attn_grouped[k].rearrange("p c t -> p (c t)")
            )
            attn_mx[k] = (codes, scales)

        def apply_attention(k):
            b, j = divmod(k, TILES)
            result_ps = psum.tile([P, S], F32, tag="result_ps")
            nc.tensor.matmul_mx(
                out=result_ps,
                lhsT=attn_mx[k][0].bitcast(FP8X4),
                lhsT_scale=attn_mx[k][1],
                rhs=v_mx[b][0].bitcast(FP8X4),
                rhs_scale=v_mx[b][1],
                start=True,
                stop=True,
            )
            result = back.tile([P, S], F32, tag="result", bufs=3)
            nc.scalar.copy(out=result, in_=result_ps)
            nc.sync.dma_start(out=out[b].rearrange("(p j) n -> p j n", j=TILES)[:, j, :], in_=result)

        def tile_stage(stage, k, *piece):
            if 0 <= k < STEPS:
                stage(k, *piece)

        def sample_stage(stage, b, *piece):
            if 0 <= b < B:
                stage(b, *piece)

        def transpose_next(b, j, half, side):
            if 2 * j + half < MAPS:
                sample_stage(transpose_map, b + 1, 2 * j + half, side)

        for step in range(-TILES - 1, STEPS + TILES):
            b, j = divmod(step, TILES)
            last = TILES - 1
            if j == 0:
                sample_stage(load_sample, b + 2)
            if j == last:
                sample_stage(regroup_x, b + 2)
            tile_stage(score_pass, step, 0)
            tile_stage(sum_gates, step - 3, 0)
            tile_stage(sum_gates, step - 3, 1)
            tile_stage(add_segment, step - 2, 2, 3)
            tile_stage(fuse, step - 4)
            tile_stage(gate_exponentials, step - 2)
            tile_stage(invert_row_sums, step - 1)
            tile_stage(score_pass, step, 1)
            tile_stage(sum_gates, step - 3, 2)
            tile_stage(sum_gates, step - 3, 3)
            tile_stage(quantise_attn, step - 4)
            tile_stage(map_weights, step - 1)
            tile_stage(score_pass, step, 2)
            transpose_next(b, j, 0, 0)
            tile_stage(log_of_gate_sum, step - 3)
            tile_stage(score_pass, step, 3)
            transpose_next(b, j, 0, 1)
            tile_stage(sum_gated, step - 3, 0)
            sample_stage(project_values, b + 1, j)
            tile_stage(invert_gate_sum, step - 3)
            tile_stage(score_pass, step, 4)
            tile_stage(apply_attention, step - 4)
            tile_stage(sum_gated, step - 3, 1)
            tile_stage(gated_maps, step - 2)
            tile_stage(score_pass, step, 5)
            transpose_next(b, j, 1, 0)
            tile_stage(sum_gated, step - 3, 2)
            tile_stage(add_segment, step - 1, 2, 1)
            tile_stage(score_pass, step, 6)
            transpose_next(b, j, 1, 1)
            tile_stage(sum_gated, step - 3, 3)
            tile_stage(add_segment, step - 1, 1, 1)
            tile_stage(add_segment, step - 1, 2, 2)
            if j == last:
                sample_stage(quantise_x, b + 2)
                sample_stage(quantise_v, b + 1)
